import numpy as np
import ml_dtypes


def mxq(x, axis, fmt="e4m3"):
    dtype, down = {"e4m3": (ml_dtypes.float8_e4m3fn, 7), "e5m2": (ml_dtypes.float8_e5m2, 14)}[fmt]
    v = np.moveaxis(np.asarray(x, np.float32).astype(ml_dtypes.bfloat16).astype(np.float64), axis, -1)
    blocks = v.reshape(v.shape[:-1] + (-1, 32))
    amax = np.abs(blocks).max(-1, keepdims=True)
    byte = np.maximum(np.where(amax > 0, np.frexp(amax)[1] - 1 + 127, 0) - down, 1)
    scale = np.exp2(byte - 127.0)
    codes = (blocks / scale).astype(np.float32).astype(dtype).astype(np.float64)
    return np.moveaxis((codes * scale).reshape(v.shape), -1, axis)


WIDE = False


def mx_kscale(k):
    if not WIDE:
        return np.ones(k)
    levels = np.array([10, -10, 5, -5, 0])
    a = np.random.permutation(np.resize(levels, k // 512 * 4)).reshape(k // 512, 4)
    idx = np.arange(k)
    return np.exp2(a[idx // 512, idx % 128 // 32])


BF16 = ml_dtypes.bfloat16


def bf(x):
    return np.asarray(x, np.float32).astype(BF16)


def f64(x):
    return np.asarray(x).astype(np.float64)


E2M1 = np.array([0.0, 0.5, 1.0, 1.5, 2.0, 3.0, 4.0, 6.0, -0.0, -0.5, -1.0, -1.5, -2.0, -3.0, -4.0, -6.0])


def pack_weight(w, fmt):
    k, n = w.shape
    w = f64(bf(w)).reshape(k // 32, 32, n)
    amax = np.abs(w).max(1)
    if fmt == "e4m3":
        byte = np.frexp(amax)[1] - 1 + 127 - 7
    else:
        mant, ex = np.frexp(amax / 6.0)
        byte = np.where(mant > 0.5, ex, ex - 1) + 127
    byte = np.clip(np.where(amax > 0, byte, 1), 1, 254)
    scaled = (w * np.exp2(127.0 - byte)[:, None, :]).reshape(k, n).astype(np.float32)
    by_word = np.ascontiguousarray(scaled.reshape(k // 512, 128, 4, n).transpose(0, 1, 3, 2))
    if fmt == "e4m3":
        words = by_word.astype(ml_dtypes.float8_e4m3fn).view(np.uint8)
    else:
        c = by_word.astype(ml_dtypes.float4_e2m1fn).view(np.uint8) & 0xF
        words = c[..., 0::2] | (c[..., 1::2] << 4)
    return np.ascontiguousarray(words), np.ascontiguousarray(byte.astype(np.uint8).reshape(k // 512, 16, n))


def unpack_weight(words, scales, fmt):
    g, p, n, _ = words.shape
    if fmt == "e4m3":
        vals = np.ascontiguousarray(words).view(ml_dtypes.float8_e4m3fn).astype(np.float64)
    else:
        nib = np.empty((g, p, n, 4), np.uint8)
        nib[..., 0::2] = words & 0xF
        nib[..., 1::2] = words >> 4
        vals = E2M1[nib]
    vals = vals * np.repeat(np.exp2(scales.astype(np.float64) - 127.0), 8, axis=1)[..., None]
    return vals.transpose(0, 1, 3, 2).reshape(g * 512, n)


B, I, H = 128, 1024, 2048
C = I + H
FMT = "e4m3"


def hard_sigmoid(v):
    return np.clip(v / 6.0 + 0.5, 0.0, 1.0)


def hard_tanh(v):
    return np.clip(v, -1.0, 1.0)


def setup_inputs():
    s = np.where(np.arange(C) < I, mx_kscale(C), 1.0)
    inputs = bf(np.random.standard_normal((B, I)) * s[:I])
    h_prev = bf(np.random.standard_normal((B, H)))
    W_z_words, W_z_scales = pack_weight(np.ascontiguousarray((np.random.standard_normal((H, C)) * 2.5 / np.sqrt(C) / s).T), FMT)
    b_z = bf(np.random.standard_normal(H) * 1.0)
    W_r_words, W_r_scales = pack_weight(np.ascontiguousarray((np.random.standard_normal((H, C)) * 2.5 / np.sqrt(C) / s).T), FMT)
    b_r = bf(np.random.standard_normal(H) * 1.0)
    W_h_words, W_h_scales = pack_weight(np.ascontiguousarray((np.random.standard_normal((H, C)) * 1.2 / np.sqrt(C) / s).T), FMT)
    b_h = bf(np.random.standard_normal(H) * 0.5)
    return {"inputs": inputs,
            "h_prev": h_prev,
            "W_z_words": W_z_words,
            "W_z_scales": W_z_scales,
            "b_z": b_z,
            "W_r_words": W_r_words,
            "W_r_scales": W_r_scales,
            "b_r": b_r,
            "W_h_words": W_h_words,
            "W_h_scales": W_h_scales,
            "b_h": b_h}


def reference(inputs, h_prev, W_z_words, W_z_scales, b_z, W_r_words, W_r_scales, b_r, W_h_words, W_h_scales, b_h):
    h = f64(h_prev)
    xq = mxq(f64(inputs), 1, "e4m3")
    ihq = np.concatenate([xq, mxq(h, 1, "e4m3")], axis=-1)
    z = hard_sigmoid((ihq @ unpack_weight(W_z_words, W_z_scales, FMT)) + f64(b_z))
    r = hard_sigmoid((ihq @ unpack_weight(W_r_words, W_r_scales, FMT)) + f64(b_r))
    irhq = np.concatenate([xq, mxq(r * h, 1, "e4m3")], axis=-1)
    h_tilde = hard_tanh((irhq @ unpack_weight(W_h_words, W_h_scales, FMT)) + f64(b_h))
    return z * h + (1.0 - z) * h_tilde

@@ -1,0 +1,252 @@
+from contextlib import ExitStack
+
+import concourse.mybir as mybir
+from concourse.masks import make_identity
+
+F32 = mybir.dt.float32
+BF16 = mybir.dt.bfloat16
+U8 = mybir.dt.uint8
+U32 = mybir.dt.uint32
+I32 = mybir.dt.int32
+FP8X4 = mybir.dt.float8_e4m3fn_x4
+ALU = mybir.AluOpType
+ACT = mybir.ActivationFunctionType
+
+P = 128
+N_IN = 1024
+N_HID = 2048
+N_CAT = N_IN + N_HID
+K_PASS = 512
+GROUPS = N_CAT // K_PASS
+X_GROUPS = N_IN // K_PASS
+CHUNK = 512
+CHUNKS = N_HID // CHUNK
+FLOPS = 2 * P * N_CAT * N_HID * 3
+
+W_R, W_Z, W_H = 0, 1, 2
+SCALES_ON_GPSIMD = False
+
+
+def plane_of(w, g):
+    i = GROUPS * w + g
+    return i // 4, 4 * (i % 4)
+
+
+def tile_grucell_w_kernel(
+    tc, inputs, h_prev, W_z_words, W_z_scales, b_z, W_r_words, W_r_scales, b_r, W_h_words, W_h_scales, b_h, out
+):
+    nc = tc.nc
+    words = (W_r_words, W_z_words, W_h_words)
+    scales = (W_r_scales, W_z_scales, W_h_scales)
+    biases = (b_r, b_z, b_h)
+
+    with ExitStack() as ctx:
+        keep = ctx.enter_context(tc.tile_pool(name="keep", bufs=1))
+        work = ctx.enter_context(tc.tile_pool(name="work", bufs=3))
+        outs = ctx.enter_context(tc.tile_pool(name="outs", bufs=4))
+        psum = ctx.enter_context(tc.psum_pool(name="psum", bufs=1))
+        ctx.enter_context(tc.manual_schedule())
+
+        def bank(i, shape, dtype, name):
+            return psum.tile(shape, dtype, tag="bank%d" % i, name=name)
+
+        xh = keep.tile([P, N_CAT], BF16, name="xh", align_bytes=64)
+        planes = keep.tile([P, 5 * N_HID], U8, name="planes", align_bytes=64)
+        w_sb = [
+            keep.tile([P, GROUPS, N_HID], U32, name="w_sb%d" % w, align_bytes=64) for w in range(3)
+        ]
+        ident_f = keep.tile([P, P], F32, name="ident_f")
+        ident_b = keep.tile([P, P], BF16, name="ident_b")
+        staging = keep.tile([P, N_HID], BF16, name="staging")
+        bias_bc = [keep.tile([P, N_HID], BF16, name="bias_bc%d" % w) for w in range(3)]
+        grouped = keep.tile([P, 4 * P * GROUPS], BF16, name="grouped", align_bytes=64)
+        xh_codes = keep.tile([P, P * GROUPS], U32, name="xh_codes", align_bytes=64)
+        xh_scales = keep.tile([P, P * GROUPS], U8, name="xh_scales", align_bytes=64)
+        rh = keep.tile([P, CHUNKS, 4, P], BF16, name="rh")
+        rh_grouped = keep.tile([P, 4 * P * CHUNKS], BF16, name="rh_grouped", align_bytes=64)
+        rh_codes = keep.tile([P, P * CHUNKS], U32, name="rh_codes", align_bytes=64)
+        rh_scales = keep.tile([P, P * CHUNKS], U8, name="rh_scales", align_bytes=64)
+        zh = keep.tile([P, N_HID], F32, name="zh")
+        omz = keep.tile([P, N_HID], F32, name="omz")
+
+        nc.vector.memset(planes[:].bitcast(I32), 0)
+        nc.vector.memset(staging[:], 0.0)
+        make_identity(nc, ident_f[:])
+        make_identity(nc, ident_b[:])
+
+        nc.sync.dma_start(out=xh[:, 0:N_IN], in_=inputs[:, :])
+        nc.sync.dma_start(out=xh[:, N_IN:N_CAT], in_=h_prev[:, :])
+        for w in range(3):
+            nc.scalar.dma_start(out=staging[w : w + 1, :], in_=biases[w].unsqueeze(0))
+
+        runs = []
+        for w in range(3):
+            for g in range(GROUPS):
+                slot, k = plane_of(w, g)
+                if runs and runs[-1][0] == w and runs[-1][2] == slot:
+                    runs[-1][4] += 1
+                else:
+                    runs.append([w, g, slot, k, 1])
+        for w, g, slot, k, cnt in runs:
+            for q in (0, 2, 1, 3):
+                dst = planes[32 * q + k : 32 * q + k + 4 * cnt, slot * N_HID : (slot + 1) * N_HID]
+                src = scales[w][g : g + cnt, 4 * q : 4 * q + 4, :]
+                if SCALES_ON_GPSIMD:
+                    nc.gpsimd.dma_start(out=dst.bitcast(F32), in_=src.bitcast(F32))
+                else:
+                    nc.sync.dma_start(out=dst.bitcast(I32), in_=src.bitcast(I32))
+
+        def load_words(w, g0, g1, n0, n1):
+            src = words[w][g0:g1].rearrange("g p n t -> p g (n t)")[:, :, 4 * n0 : 4 * n1]
+            nc.sync.dma_start(out=w_sb[w][:, g0:g1, n0:n1].bitcast(I32), in_=src.bitcast(I32))
+
+        for g in range(GROUPS):
+            load_words(W_R, g, g + 1, 0, N_HID)
+        for g in range(4):
+            load_words(W_Z, g, g + 1, 0, N_HID)
+        for half in range(2):
+            load_words(W_Z, 4, 6, half * 1024, (half + 1) * 1024)
+        for g in range(X_GROUPS):
+            load_words(W_H, g, g + 1, 0, N_HID)
+        for c in range(CHUNKS):
+            load_words(W_H, X_GROUPS, GROUPS, c * CHUNK, (c + 1) * CHUNK)
+
+        xw = xh[:].bitcast(F32)
+        gw = grouped[:].bitcast(F32)
+        pts = []
+        for j in range(3):
+            pt = bank(4 + j, [P, 2, 2, P], F32, "pt%d" % j)
+            for gg in range(2):
+                g = 2 * j + gg
+                for u in range(2):
+                    nc.tensor.transpose(pt[:, gg, u, :], xw[:, 256 * g + u : 256 * (g + 1) : 2], ident_f[:])
+            pts.append(pt)
+
+        def copy_xh(j):
+            nc.vector.tensor_copy(
+                out=gw[:, 512 * j : 512 * (j + 1)].rearrange("p (g r u) -> p g r u", g=2, u=2),
+                in_=pts[j][:].rearrange("p g u r -> p g r u"),
+            )
+
+        def quant_xh(j):
+            nc.vector.quantize_mx(
+                out=xh_codes[:, 256 * j : 256 * (j + 1)].bitcast(FP8X4),
+                scales=xh_scales[:, 256 * j : 256 * (j + 1)],
+                in_=grouped[:, 1024 * j : 1024 * (j + 1)],
+            )
+
+        copy_xh(0)
+        copy_xh(1)
+        quant_xh(0)
+        copy_xh(2)
+        quant_xh(1)
+        quant_xh(2)
+
+        bias_banks = (7, 4, 5, 6, 7, 4)
+        for w in range(3):
+            for half in range(2):
+                pb = bank(bias_banks[2 * w + half], [P, 1024], BF16, "pb%d_%d" % (w, half))
+                for s in range(2):
+                    col = 1024 * half + 512 * s
+                    nc.tensor.matmul(
+                        out=pb[:, 512 * s : 512 * (s + 1)],
+                        lhsT=ident_b[:, w : w + 1].to_broadcast([P, P]),
+                        rhs=staging[:, col : col + 512],
+                        start=True,
+                        stop=True,
+                    )
+                nc.scalar.copy(out=bias_bc[w][:, 1024 * half : 1024 * (half + 1)], in_=pb[:])
+
+        def mx_pass(acc, w, g, c, start, stop):
+            slot, k = plane_of(w, g)
+            if w == W_H and g >= X_GROUPS:
+                codes, scl, col = rh_codes, rh_scales, P * (g - X_GROUPS)
+            else:
+                codes, scl, col = xh_codes, xh_scales, P * g
+            nc.tensor.matmul_mx(
+                out=acc[:],
+                lhsT=codes[:, col : col + P].bitcast(FP8X4),
+                lhsT_scale=scl[:, col : col + P],
+                rhs=w_sb[w][:, g, c * CHUNK : (c + 1) * CHUNK].bitcast(FP8X4),
+                rhs_scale=planes[k:P, slot * N_HID + c * CHUNK : slot * N_HID + (c + 1) * CHUNK],
+                start=start,
+                stop=stop,
+            )
+
+        def gate6(acc, w, c):
+            t = work.tile([P, CHUNK], F32, name="t")
+            nc.vector.scalar_tensor_tensor(
+                out=t[:], in0=acc[:], scalar=3.0, in1=bias_bc[w][:, c * CHUNK : (c + 1) * CHUNK],
+                op0=ALU.add, op1=ALU.add,
+            )
+            nc.vector.tensor_scalar(out=t[:], in0=t[:], scalar1=0.0, scalar2=6.0, op0=ALU.max, op1=ALU.min)
+            return t
+
+        r_acc = [bank(c, [P, CHUNK], F32, "r_acc%d" % c) for c in range(CHUNKS)]
+        for g in range(GROUPS):
+            for c in range(CHUNKS):
+                mx_pass(r_acc[c], W_R, g, c, g == 0, g == GROUPS - 1)
+
+        z_acc = [bank(4 + c, [P, CHUNK], F32, "z_acc%d" % c) for c in range(CHUNKS)]
+
+        def quant_rh(c):
+            nc.vector.quantize_mx(
+                out=rh_codes[:, P * c : P * (c + 1)].bitcast(FP8X4),
+                scales=rh_scales[:, P * c : P * (c + 1)],
+                in_=rh_grouped[:, 512 * c : 512 * (c + 1)],
+            )
+
+        for c in range(CHUNKS):
+            t = gate6(r_acc[c], W_R, c)
+            nc.vector.scalar_tensor_tensor(
+                out=rh[:, c],
+                in0=t[:].rearrange("p (m t) -> p t m", t=4),
+                scalar=1.0 / 6.0,
+                in1=xh[:, N_IN + c * CHUNK : N_IN + (c + 1) * CHUNK].rearrange("p (m t) -> p t m", t=4),
+                op0=ALU.mult,
+                op1=ALU.mult,
+            )
+            if c >= 1:
+                quant_rh(c - 1)
+            for cc in range(CHUNKS):
+                mx_pass(z_acc[cc], W_Z, c, cc, c == 0, False)
+            prh = bank(c, [P, 4, P], BF16, "prh%d" % c)
+            for t4 in range(4):
+                nc.tensor.transpose(prh[:, t4, :], rh[:, c, t4, :], ident_b[:])
+            nc.scalar.copy(
+                out=rh_grouped[:, 512 * c : 512 * (c + 1)].rearrange("p (r t) -> p r t", t=4),
+                in_=prh[:].rearrange("p t r -> p r t"),
+            )
+        quant_rh(CHUNKS - 1)
+
+        def z_epilogue(c):
+            cols = slice(c * CHUNK, (c + 1) * CHUNK)
+            t = gate6(z_acc[c], W_Z, c)
+            nc.vector.scalar_tensor_tensor(
+                out=zh[:, cols], in0=t[:], scalar=1.0 / 6.0, in1=xh[:, N_IN + c * CHUNK : N_IN + (c + 1) * CHUNK],
+                op0=ALU.mult, op1=ALU.mult,
+            )
+            nc.scalar.activation(out=omz[:, cols], in_=t[:], func=ACT.Copy, bias=1.0, scale=-1.0 / 6.0)
+
+        for half in range(2):
+            for c in (2 * half, 2 * half + 1):
+                mx_pass(z_acc[c], W_Z, 4, c, False, False)
+                mx_pass(z_acc[c], W_Z, 5, c, False, True)
+            for c in (2 * half, 2 * half + 1):
+                z_epilogue(c)
+
+        h_acc = [bank(c, [P, CHUNK], F32, "h_acc%d" % c) for c in range(CHUNKS)]
+        for g in range(X_GROUPS):
+            for c in range(CHUNKS):
+                mx_pass(h_acc[c], W_H, g, c, g == 0, False)
+        for c in range(CHUNKS):
+            cols = slice(c * CHUNK, (c + 1) * CHUNK)
+            for g in range(X_GROUPS, GROUPS):
+                mx_pass(h_acc[c], W_H, g, c, False, g == GROUPS - 1)
+            t = work.tile([P, CHUNK], F32, name="t")
+            o = outs.tile([P, CHUNK], F32, name="o")
+            nc.vector.tensor_tensor(out=t[:], in0=h_acc[c][:], in1=bias_bc[W_H][:, cols], op=ALU.add)
+            nc.vector.tensor_scalar(out=t[:], in0=t[:], scalar1=-1.0, scalar2=1.0, op0=ALU.max, op1=ALU.min)
+            nc.vector.tensor_tensor(out=t[:], in0=t[:], in1=omz[:, cols], op=ALU.mult)
+            nc.vector.tensor_tensor(out=o[:], in0=t[:], in1=zh[:, cols], op=ALU.add)
+            nc.sync.dma_start(out=out[:, cols], in_=o[:])

@@ -24,7 +24,7 @@ CHUNKS = N_HID // CHUNK
 FLOPS = 2 * P * N_CAT * N_HID * 3
 
 W_R, W_Z, W_H = 0, 1, 2
-SCALES_ON_GPSIMD = False
+SCALES_ON_GPSIMD = True
 
 
 def plane_of(w, g):

@@ -43,7 +43,7 @@ def tile_grucell_w_kernel(
     with ExitStack() as ctx:
         keep = ctx.enter_context(tc.tile_pool(name="keep", bufs=1))
         work = ctx.enter_context(tc.tile_pool(name="work", bufs=3))
-        outs = ctx.enter_context(tc.tile_pool(name="outs", bufs=4))
+        outs = ctx.enter_context(tc.tile_pool(name="outs", bufs=3))
         psum = ctx.enter_context(tc.psum_pool(name="psum", bufs=1))
         ctx.enter_context(tc.manual_schedule())
 
@@ -57,16 +57,16 @@ def tile_grucell_w_kernel(
         ]
         ident_f = keep.tile([P, P], F32, name="ident_f")
         ident_b = keep.tile([P, P], BF16, name="ident_b")
-        staging = keep.tile([P, N_HID], BF16, name="staging")
+        staging = keep.tile([P, N_HID], BF16, name="staging", tag="stage_rh")
         bias_bc = [keep.tile([P, N_HID], BF16, name="bias_bc%d" % w) for w in range(3)]
         grouped = keep.tile([P, 4 * P * GROUPS], BF16, name="grouped", align_bytes=64)
         xh_codes = keep.tile([P, P * GROUPS], U32, name="xh_codes", align_bytes=64)
         xh_scales = keep.tile([P, P * GROUPS], U8, name="xh_scales", align_bytes=64)
-        rh = keep.tile([P, CHUNKS, 4, P], BF16, name="rh")
-        rh_grouped = keep.tile([P, 4 * P * CHUNKS], BF16, name="rh_grouped", align_bytes=64)
+        rh_grouped = grouped
         rh_codes = keep.tile([P, P * CHUNKS], U32, name="rh_codes", align_bytes=64)
         rh_scales = keep.tile([P, P * CHUNKS], U8, name="rh_scales", align_bytes=64)
-        zh = keep.tile([P, N_HID], F32, name="zh")
+        hp1 = keep.tile([P, N_HID], F32, name="hp1")
+        zhp = keep.tile([P, N_HID], F32, name="zhp")
         omz = keep.tile([P, N_HID], F32, name="omz")
 
         nc.vector.memset(planes[:].bitcast(I32), 0)
@@ -102,10 +102,8 @@ def tile_grucell_w_kernel(
 
         for g in range(GROUPS):
             load_words(W_R, g, g + 1, 0, N_HID)
-        for g in range(4):
+        for g in range(GROUPS):
             load_words(W_Z, g, g + 1, 0, N_HID)
-        for half in range(2):
-            load_words(W_Z, 4, 6, half * 1024, (half + 1) * 1024)
         for g in range(X_GROUPS):
             load_words(W_H, g, g + 1, 0, N_HID)
         for c in range(CHUNKS):
@@ -173,80 +171,153 @@ def tile_grucell_w_kernel(
                 stop=stop,
             )
 
-        def gate6(acc, w, c):
+        def cols_of(c):
+            return slice(c * CHUNK, (c + 1) * CHUNK)
+
+        def add_bias(acc, w, c, shift):
             t = work.tile([P, CHUNK], F32, name="t")
             nc.vector.scalar_tensor_tensor(
-                out=t[:], in0=acc[:], scalar=3.0, in1=bias_bc[w][:, c * CHUNK : (c + 1) * CHUNK],
-                op0=ALU.add, op1=ALU.add,
+                out=t[:], in0=acc[:], scalar=shift, in1=bias_bc[w][:, cols_of(c)], op0=ALU.add, op1=ALU.add
             )
-            nc.vector.tensor_scalar(out=t[:], in0=t[:], scalar1=0.0, scalar2=6.0, op0=ALU.max, op1=ALU.min)
             return t
+
+        nc.scalar.activation(out=hp1[:], in_=xh[:, N_IN:N_CAT], func=ACT.Copy, bias=1.0, scale=1.0)
 
         r_acc = [bank(c, [P, CHUNK], F32, "r_acc%d" % c) for c in range(CHUNKS)]
         for g in range(GROUPS):
             for c in range(CHUNKS):
                 mx_pass(r_acc[c], W_R, g, c, g == 0, g == GROUPS - 1)
 
+        rh = keep.tile([P, CHUNKS, 4, P], BF16, name="rh", tag="stage_rh")
         z_acc = [bank(4 + c, [P, CHUNK], F32, "z_acc%d" % c) for c in range(CHUNKS)]
+        r_a = {}
+        prh = {}
 
-        def quant_rh(c):
+        def r_front(c):
+            t = add_bias(r_acc[c], W_R, c, 3.0)
+            a = work.tile([P, 4, P], F32, name="a")
+            nc.scalar.activation(
+                out=a[:], in_=t[:].rearrange("p (m t) -> p t m", t=4), func=ACT.Relu, scale=1.0 / 6.0
+            )
+            r_a[c] = a
+
+        def r_back(c):
+            nc.vector.scalar_tensor_tensor(
+                out=rh[:, c],
+                in0=r_a[c][:],
+                scalar=1.0,
+                in1=xh[:, N_IN + c * CHUNK : N_IN + (c + 1) * CHUNK].rearrange("p (m t) -> p t m", t=4),
+                op0=ALU.min,
+                op1=ALU.mult,
+            )
+
+        def z_group(g):
+            for cc in range(CHUNKS):
+                mx_pass(z_acc[cc], W_Z, g, cc, g == 0, g == GROUPS - 1)
+
+        def rh_transpose(c):
+            prh[c] = bank(c, [P, 4, P], BF16, "prh%d" % c)
+            for t4 in range(4):
+                nc.tensor.transpose(prh[c][:, t4, :], rh[:, c, t4, :], ident_b[:])
+
+        def rh_copy(c):
+            nc.scalar.copy(
+                out=rh_grouped[:, 512 * c : 512 * (c + 1)].rearrange("p (r t) -> p r t", t=4),
+                in_=prh[c][:].rearrange("p t r -> p r t"),
+            )
+
+        def rh_quant(c):
             nc.vector.quantize_mx(
                 out=rh_codes[:, P * c : P * (c + 1)].bitcast(FP8X4),
                 scales=rh_scales[:, P * c : P * (c + 1)],
                 in_=rh_grouped[:, 512 * c : 512 * (c + 1)],
             )
 
-        for c in range(CHUNKS):
-            t = gate6(r_acc[c], W_R, c)
-            nc.vector.scalar_tensor_tensor(
-                out=rh[:, c],
-                in0=t[:].rearrange("p (m t) -> p t m", t=4),
-                scalar=1.0 / 6.0,
-                in1=xh[:, N_IN + c * CHUNK : N_IN + (c + 1) * CHUNK].rearrange("p (m t) -> p t m", t=4),
-                op0=ALU.mult,
-                op1=ALU.mult,
-            )
-            if c >= 1:
-                quant_rh(c - 1)
-            for cc in range(CHUNKS):
-                mx_pass(z_acc[cc], W_Z, c, cc, c == 0, False)
-            prh = bank(c, [P, 4, P], BF16, "prh%d" % c)
-            for t4 in range(4):
-                nc.tensor.transpose(prh[:, t4, :], rh[:, c, t4, :], ident_b[:])
-            nc.scalar.copy(
-                out=rh_grouped[:, 512 * c : 512 * (c + 1)].rearrange("p (r t) -> p r t", t=4),
-                in_=prh[:].rearrange("p t r -> p r t"),
-            )
-        quant_rh(CHUNKS - 1)
+        r_front(0)
+        r_front(1)
+        r_back(0)
+        z_group(0)
+        rh_transpose(0)
+        r_front(2)
+        rh_copy(0)
+        r_back(1)
+        z_group(1)
+        rh_transpose(1)
+        r_front(3)
+        rh_copy(1)
+        r_back(2)
+        rh_quant(0)
+        z_group(2)
+        rh_transpose(2)
+        rh_copy(2)
+        r_back(3)
+        rh_quant(1)
+        z_group(3)
+        rh_transpose(3)
+        rh_copy(3)
+        rh_quant(2)
+        rh_quant(3)
+        z_group(4)
+        z_group(5)
 
-        def z_epilogue(c):
-            cols = slice(c * CHUNK, (c + 1) * CHUNK)
-            t = gate6(z_acc[c], W_Z, c)
-            nc.vector.scalar_tensor_tensor(
-                out=zh[:, cols], in0=t[:], scalar=1.0 / 6.0, in1=xh[:, N_IN + c * CHUNK : N_IN + (c + 1) * CHUNK],
-                op0=ALU.mult, op1=ALU.mult,
-            )
-            nc.scalar.activation(out=omz[:, cols], in_=t[:], func=ACT.Copy, bias=1.0, scale=-1.0 / 6.0)
+        z_a = {}
 
-        for half in range(2):
-            for c in (2 * half, 2 * half + 1):
-                mx_pass(z_acc[c], W_Z, 4, c, False, False)
-                mx_pass(z_acc[c], W_Z, 5, c, False, True)
-            for c in (2 * half, 2 * half + 1):
-                z_epilogue(c)
+        def z_front(c):
+            t = add_bias(z_acc[c], W_Z, c, 3.0)
+            a = work.tile([P, CHUNK], F32, name="a")
+            nc.scalar.activation(out=a[:], in_=t[:], func=ACT.Relu, scale=1.0 / 6.0)
+            z_a[c] = a
+
+        def z_back(c):
+            nc.vector.scalar_tensor_tensor(
+                out=zhp[:, cols_of(c)], in0=z_a[c][:], scalar=1.0, in1=hp1[:, cols_of(c)], op0=ALU.min, op1=ALU.mult
+            )
+            nc.scalar.activation(out=omz[:, cols_of(c)], in_=z_a[c][:], func=ACT.Relu, bias=1.0, scale=-1.0)
+
+        z_front(0)
+        z_front(1)
+        z_back(0)
+        z_front(2)
+        z_back(1)
+        z_front(3)
+        z_back(2)
+        z_back(3)
 
         h_acc = [bank(c, [P, CHUNK], F32, "h_acc%d" % c) for c in range(CHUNKS)]
         for g in range(X_GROUPS):
             for c in range(CHUNKS):
                 mx_pass(h_acc[c], W_H, g, c, g == 0, False)
-        for c in range(CHUNKS):
-            cols = slice(c * CHUNK, (c + 1) * CHUNK)
+        h_a = {}
+
+        def h_front(c):
             for g in range(X_GROUPS, GROUPS):
                 mx_pass(h_acc[c], W_H, g, c, False, g == GROUPS - 1)
-            t = work.tile([P, CHUNK], F32, name="t")
+            t = add_bias(h_acc[c], W_H, c, 1.0)
+            a = work.tile([P, CHUNK], F32, name="a")
+            nc.scalar.activation(out=a[:], in_=t[:], func=ACT.Relu)
+            h_a[c] = a
+
+        def h_mid(c):
+            nc.vector.scalar_tensor_tensor(
+                out=h_a[c][:], in0=h_a[c][:], scalar=2.0, in1=omz[:, cols_of(c)], op0=ALU.min, op1=ALU.mult
+            )
+
+        def h_back(c):
             o = outs.tile([P, CHUNK], F32, name="o")
-            nc.vector.tensor_tensor(out=t[:], in0=h_acc[c][:], in1=bias_bc[W_H][:, cols], op=ALU.add)
-            nc.vector.tensor_scalar(out=t[:], in0=t[:], scalar1=-1.0, scalar2=1.0, op0=ALU.max, op1=ALU.min)
-            nc.vector.tensor_tensor(out=t[:], in0=t[:], in1=omz[:, cols], op=ALU.mult)
-            nc.vector.tensor_tensor(out=o[:], in0=t[:], in1=zh[:, cols], op=ALU.add)
-            nc.sync.dma_start(out=out[:, cols], in_=o[:])
+            nc.vector.scalar_tensor_tensor(
+                out=o[:], in0=h_a[c][:], scalar=-1.0, in1=zhp[:, cols_of(c)], op0=ALU.add, op1=ALU.add
+            )
+            nc.sync.dma_start(out=out[:, cols_of(c)], in_=o[:])
+
+        h_front(0)
+        h_front(1)
+        h_mid(0)
+        h_back(0)
+        h_front(2)
+        h_mid(1)
+        h_back(1)
+        h_front(3)
+        h_mid(2)
+        h_mid(3)
+        h_back(2)
+        h_back(3)

@@ -24,6 +24,8 @@ CHUNKS = N_HID // CHUNK
 FLOPS = 2 * P * N_CAT * N_HID * 3
 
 W_R, W_Z, W_H = 0, 1, 2
+H_CHUNKS = ((0, 512), (512, 512), (1024, 512), (1536, 256), (1792, 256))
+H_PIECES = ((0, 0, 512), (1, 512, 512), (2, 1024, 512), (3, 1536, 256), (4, 1792, 128), (4, 1920, 128))
 SCALES_ON_GPSIMD = True
 
 
@@ -43,7 +45,6 @@ def tile_grucell_w_kernel(
     with ExitStack() as ctx:
         keep = ctx.enter_context(tc.tile_pool(name="keep", bufs=1))
         work = ctx.enter_context(tc.tile_pool(name="work", bufs=3))
-        outs = ctx.enter_context(tc.tile_pool(name="outs", bufs=3))
         psum = ctx.enter_context(tc.psum_pool(name="psum", bufs=1))
         ctx.enter_context(tc.manual_schedule())
 
@@ -106,8 +107,11 @@ def tile_grucell_w_kernel(
             load_words(W_Z, g, g + 1, 0, N_HID)
         for g in range(X_GROUPS):
             load_words(W_H, g, g + 1, 0, N_HID)
-        for c in range(CHUNKS):
-            load_words(W_H, X_GROUPS, GROUPS, c * CHUNK, (c + 1) * CHUNK)
+        for n0, width in H_CHUNKS[:-1]:
+            load_words(W_H, X_GROUPS, GROUPS, n0, n0 + width)
+        n0, width = H_CHUNKS[-1]
+        load_words(W_H, X_GROUPS, GROUPS - 1, n0, n0 + width)
+        load_words(W_H, GROUPS - 1, GROUPS, n0, n0 + width)
 
         xw = xh[:].bitcast(F32)
         gw = grouped[:].bitcast(F32)
@@ -156,6 +160,9 @@ def tile_grucell_w_kernel(
                 nc.scalar.copy(out=bias_bc[w][:, 1024 * half : 1024 * (half + 1)], in_=pb[:])
 
         def mx_pass(acc, w, g, c, start, stop):
+            mx_cols(acc, w, g, c * CHUNK, CHUNK, start, stop)
+
+        def mx_cols(acc, w, g, n0, width, start, stop):
             slot, k = plane_of(w, g)
             if w == W_H and g >= X_GROUPS:
                 codes, scl, col = rh_codes, rh_scales, P * (g - X_GROUPS)
@@ -165,8 +172,8 @@ def tile_grucell_w_kernel(
                 out=acc[:],
                 lhsT=codes[:, col : col + P].bitcast(FP8X4),
                 lhsT_scale=scl[:, col : col + P],
-                rhs=w_sb[w][:, g, c * CHUNK : (c + 1) * CHUNK].bitcast(FP8X4),
-                rhs_scale=planes[k:P, slot * N_HID + c * CHUNK : slot * N_HID + (c + 1) * CHUNK],
+                rhs=w_sb[w][:, g, n0 : n0 + width].bitcast(FP8X4),
+                rhs_scale=planes[k:P, slot * N_HID + n0 : slot * N_HID + n0 + width],
                 start=start,
                 stop=stop,
             )
@@ -283,41 +290,70 @@ def tile_grucell_w_kernel(
         z_back(2)
         z_back(3)
 
-        h_acc = [bank(c, [P, CHUNK], F32, "h_acc%d" % c) for c in range(CHUNKS)]
+        h_acc = [bank(i, [P, width], F32, "h_acc%d" % i) for i, (n0, width) in enumerate(H_CHUNKS)]
         for g in range(X_GROUPS):
-            for c in range(CHUNKS):
-                mx_pass(h_acc[c], W_H, g, c, g == 0, False)
+            for i, (n0, width) in enumerate(H_CHUNKS):
+                mx_cols(h_acc[i], W_H, g, n0, width, g == 0, False)
         h_a = {}
 
-        def h_front(c):
+        def h_passes(i):
+            n0, width = H_CHUNKS[i]
             for g in range(X_GROUPS, GROUPS):
-                mx_pass(h_acc[c], W_H, g, c, False, g == GROUPS - 1)
-            t = add_bias(h_acc[c], W_H, c, 1.0)
-            a = work.tile([P, CHUNK], F32, name="a")
+                mx_cols(h_acc[i], W_H, g, n0, width, False, g == GROUPS - 1)
+
+        def h_front(j):
+            i, n0, width = H_PIECES[j]
+            off = n0 - H_CHUNKS[i][0]
+            t = work.tile([P, width], F32, name="t")
+            nc.vector.scalar_tensor_tensor(
+                out=t[:], in0=h_acc[i][:, off : off + width], scalar=1.0, in1=bias_bc[W_H][:, n0 : n0 + width],
+                op0=ALU.add, op1=ALU.add
+            )
+            a = work.tile([P, width], F32, name="a")
             nc.scalar.activation(out=a[:], in_=t[:], func=ACT.Relu)
-            h_a[c] = a
+            h_a[j] = a
 
-        def h_mid(c):
+        def h_mid(j):
+            i, n0, width = H_PIECES[j]
             nc.vector.scalar_tensor_tensor(
-                out=h_a[c][:], in0=h_a[c][:], scalar=2.0, in1=omz[:, cols_of(c)], op0=ALU.min, op1=ALU.mult
+                out=h_a[j][:], in0=h_a[j][:], scalar=2.0, in1=omz[:, n0 : n0 + width], op0=ALU.min, op1=ALU.mult
             )
 
-        def h_back(c):
-            o = outs.tile([P, CHUNK], F32, name="o")
+        def h_back(j):
+            i, n0, width = H_PIECES[j]
             nc.vector.scalar_tensor_tensor(
-                out=o[:], in0=h_a[c][:], scalar=-1.0, in1=zhp[:, cols_of(c)], op0=ALU.add, op1=ALU.add
+                out=zhp[:, n0 : n0 + width], in0=h_a[j][:], scalar=-1.0, in1=zhp[:, n0 : n0 + width],
+                op0=ALU.add, op1=ALU.add
             )
-            nc.sync.dma_start(out=out[:, cols_of(c)], in_=o[:])
 
+        def h_store(n0, width):
+            nc.sync.dma_start(out=out[:, n0 : n0 + width], in_=zhp[:, n0 : n0 + width])
+
+        h_passes(0)
         h_front(0)
+        h_passes(1)
         h_front(1)
         h_mid(0)
         h_back(0)
+        h_store(0, 512)
+        h_passes(2)
         h_front(2)
         h_mid(1)
         h_back(1)
+        h_store(512, 512)
+        h_passes(3)
         h_front(3)
         h_mid(2)
-        h_mid(3)
         h_back(2)
+        h_store(1024, 512)
+        h_mid(3)
         h_back(3)
+        h_store(1536, 256)
+        h_passes(4)
+        h_front(4)
+        h_front(5)
+        h_mid(4)
+        h_mid(5)
+        h_back(4)
+        h_back(5)
+        h_store(1792, 256)

@@ -25,8 +25,15 @@ FLOPS = 2 * P * N_CAT * N_HID * 3
 
 W_R, W_Z, W_H = 0, 1, 2
 H_CHUNKS = ((0, 512), (512, 512), (1024, 512), (1536, 256), (1792, 256))
-H_PIECES = ((0, 0, 512), (1, 512, 512), (2, 1024, 512), (3, 1536, 256), (4, 1792, 128), (4, 1920, 128))
-SCALES_ON_GPSIMD = True
+H_LOADS = (
+    (0, 6, 0, 512), (0, 6, 512, 1024), (0, 4, 1024, 1536), (4, 6, 1024, 1536),
+    (0, 5, 1536, 2048), (5, 6, 1536, 1792), (5, 6, 1792, 2048),
+)
+H_PIECES = (
+    (0, 0, 256), (0, 256, 256), (1, 512, 256), (1, 768, 256), (2, 1024, 256), (2, 1280, 256),
+    (3, 1536, 256), (4, 1792, 256),
+)
+SCALES_ON_GPSIMD = False
 
 
 def plane_of(w, g):
@@ -105,13 +112,8 @@ def tile_grucell_w_kernel(
             load_words(W_R, g, g + 1, 0, N_HID)
         for g in range(GROUPS):
             load_words(W_Z, g, g + 1, 0, N_HID)
-        for g in range(X_GROUPS):
-            load_words(W_H, g, g + 1, 0, N_HID)
-        for n0, width in H_CHUNKS[:-1]:
-            load_words(W_H, X_GROUPS, GROUPS, n0, n0 + width)
-        n0, width = H_CHUNKS[-1]
-        load_words(W_H, X_GROUPS, GROUPS - 1, n0, n0 + width)
-        load_words(W_H, GROUPS - 1, GROUPS, n0, n0 + width)
+        for g0, g1, n0, n1 in H_LOADS:
+            load_words(W_H, g0, g1, n0, n1)
 
         xw = xh[:].bitcast(F32)
         gw = grouped[:].bitcast(F32)
@@ -291,15 +293,13 @@ def tile_grucell_w_kernel(
         z_back(3)
 
         h_acc = [bank(i, [P, width], F32, "h_acc%d" % i) for i, (n0, width) in enumerate(H_CHUNKS)]
-        for g in range(X_GROUPS):
-            for i, (n0, width) in enumerate(H_CHUNKS):
-                mx_cols(h_acc[i], W_H, g, n0, width, g == 0, False)
         h_a = {}
 
-        def h_passes(i):
-            n0, width = H_CHUNKS[i]
-            for g in range(X_GROUPS, GROUPS):
-                mx_cols(h_acc[i], W_H, g, n0, width, False, g == GROUPS - 1)
+        def h_passes(chunks):
+            for g in range(GROUPS):
+                for i in chunks:
+                    n0, width = H_CHUNKS[i]
+                    mx_cols(h_acc[i], W_H, g, n0, width, g == 0, g == GROUPS - 1)
 
         def h_front(j):
             i, n0, width = H_PIECES[j]
@@ -329,31 +329,12 @@ def tile_grucell_w_kernel(
         def h_store(n0, width):
             nc.sync.dma_start(out=out[:, n0 : n0 + width], in_=zhp[:, n0 : n0 + width])
 
-        h_passes(0)
-        h_front(0)
-        h_passes(1)
-        h_front(1)
-        h_mid(0)
-        h_back(0)
-        h_store(0, 512)
-        h_passes(2)
-        h_front(2)
-        h_mid(1)
-        h_back(1)
-        h_store(512, 512)
-        h_passes(3)
-        h_front(3)
-        h_mid(2)
-        h_back(2)
-        h_store(1024, 512)
-        h_mid(3)
-        h_back(3)
-        h_store(1536, 256)
-        h_passes(4)
-        h_front(4)
-        h_front(5)
-        h_mid(4)
-        h_mid(5)
-        h_back(4)
-        h_back(5)
-        h_store(1792, 256)
+        for i in range(4):
+            h_passes((i,) if i < 3 else (3, 4))
+            h_front(2 * i)
+            h_front(2 * i + 1)
+            h_mid(2 * i)
+            h_mid(2 * i + 1)
+            h_back(2 * i)
+            h_back(2 * i + 1)
+            h_store(512 * i, 512)

@@ -108,10 +108,10 @@ def tile_grucell_w_kernel(
             src = words[w][g0:g1].rearrange("g p n t -> p g (n t)")[:, :, 4 * n0 : 4 * n1]
             nc.sync.dma_start(out=w_sb[w][:, g0:g1, n0:n1].bitcast(I32), in_=src.bitcast(I32))
 
-        for g in range(GROUPS):
-            load_words(W_R, g, g + 1, 0, N_HID)
-        for g in range(GROUPS):
-            load_words(W_Z, g, g + 1, 0, N_HID)
+        for g0, g1 in ((0, 3), (3, 6)):
+            load_words(W_R, g0, g1, 0, N_HID)
+        for g0, g1 in ((0, 3), (3, 5), (5, 6)):
+            load_words(W_Z, g0, g1, 0, N_HID)
         for g0, g1, n0, n1 in H_LOADS:
             load_words(W_H, g0, g1, n0, n1)
 

from contextlib import ExitStack

import concourse.mybir as mybir
from concourse.masks import make_identity

F32 = mybir.dt.float32
BF16 = mybir.dt.bfloat16
U8 = mybir.dt.uint8
U32 = mybir.dt.uint32
I32 = mybir.dt.int32
FP8X4 = mybir.dt.float8_e4m3fn_x4
ALU = mybir.AluOpType
ACT = mybir.ActivationFunctionType

P = 128
N_IN = 1024
N_HID = 2048
N_CAT = N_IN + N_HID
K_PASS = 512
GROUPS = N_CAT // K_PASS
X_GROUPS = N_IN // K_PASS
CHUNK = 512
CHUNKS = N_HID // CHUNK
FLOPS = 2 * P * N_CAT * N_HID * 3

W_R, W_Z, W_H = 0, 1, 2
H_CHUNKS = ((0, 512), (512, 512), (1024, 512), (1536, 256), (1792, 256))
H_LOADS = (
    (0, 6, 0, 512), (0, 6, 512, 1024), (0, 4, 1024, 1536), (4, 6, 1024, 1536),
    (0, 5, 1536, 2048), (5, 6, 1536, 1792), (5, 6, 1792, 2048),
)
H_PIECES = (
    (0, 0, 256), (0, 256, 256), (1, 512, 256), (1, 768, 256), (2, 1024, 256), (2, 1280, 256),
    (3, 1536, 256), (4, 1792, 256),
)
SCALES_ON_GPSIMD = False


def plane_of(w, g):
    i = GROUPS * w + g
    return i // 4, 4 * (i % 4)


def tile_grucell_w_kernel(
    tc, inputs, h_prev, W_z_words, W_z_scales, b_z, W_r_words, W_r_scales, b_r, W_h_words, W_h_scales, b_h, out
):
    nc = tc.nc
    words = (W_r_words, W_z_words, W_h_words)
    scales = (W_r_scales, W_z_scales, W_h_scales)
    biases = (b_r, b_z, b_h)

    with ExitStack() as ctx:
        keep = ctx.enter_context(tc.tile_pool(name="keep", bufs=1))
        work = ctx.enter_context(tc.tile_pool(name="work", bufs=3))
        psum = ctx.enter_context(tc.psum_pool(name="psum", bufs=1))
        ctx.enter_context(tc.manual_schedule())

        def bank(i, shape, dtype, name):
            return psum.tile(shape, dtype, tag="bank%d" % i, name=name)

        xh = keep.tile([P, N_CAT], BF16, name="xh", align_bytes=64)
        planes = keep.tile([P, 5 * N_HID], U8, name="planes", align_bytes=64)
        w_sb = [
            keep.tile([P, GROUPS, N_HID], U32, name="w_sb%d" % w, align_bytes=64) for w in range(3)
        ]
        ident_f = keep.tile([P, P], F32, name="ident_f")
        ident_b = keep.tile([P, P], BF16, name="ident_b")
        staging = keep.tile([P, N_HID], BF16, name="staging", tag="stage_rh")
        bias_bc = [keep.tile([P, N_HID], BF16, name="bias_bc%d" % w) for w in range(3)]
        grouped = keep.tile([P, 4 * P * GROUPS], BF16, name="grouped", align_bytes=64)
        xh_codes = keep.tile([P, P * GROUPS], U32, name="xh_codes", align_bytes=64)
        xh_scales = keep.tile([P, P * GROUPS], U8, name="xh_scales", align_bytes=64)
        rh_grouped = grouped
        rh_codes = keep.tile([P, P * CHUNKS], U32, name="rh_codes", align_bytes=64)
        rh_scales = keep.tile([P, P * CHUNKS], U8, name="rh_scales", align_bytes=64)
        hp1 = keep.tile([P, N_HID], F32, name="hp1")
        zhp = keep.tile([P, N_HID], F32, name="zhp")
        omz = keep.tile([P, N_HID], F32, name="omz")

        nc.vector.memset(planes[:].bitcast(I32), 0)
        nc.vector.memset(staging[:], 0.0)
        make_identity(nc, ident_f[:])
        make_identity(nc, ident_b[:])

        nc.sync.dma_start(out=xh[:, 0:N_IN], in_=inputs[:, :])
        nc.sync.dma_start(out=xh[:, N_IN:N_CAT], in_=h_prev[:, :])
        for w in range(3):
            nc.scalar.dma_start(out=staging[w : w + 1, :], in_=biases[w].unsqueeze(0))

        runs = []
        for w in range(3):
            for g in range(GROUPS):
                slot, k = plane_of(w, g)
                if runs and runs[-1][0] == w and runs[-1][2] == slot:
                    runs[-1][4] += 1
                else:
                    runs.append([w, g, slot, k, 1])
        for w, g, slot, k, cnt in runs:
            for q in (0, 2, 1, 3):
                dst = planes[32 * q + k : 32 * q + k + 4 * cnt, slot * N_HID : (slot + 1) * N_HID]
                src = scales[w][g : g + cnt, 4 * q : 4 * q + 4, :]
                if SCALES_ON_GPSIMD:
                    nc.gpsimd.dma_start(out=dst.bitcast(F32), in_=src.bitcast(F32))
                else:
                    nc.sync.dma_start(out=dst.bitcast(I32), in_=src.bitcast(I32))

        def load_words(w, g0, g1, n0, n1):
            src = words[w][g0:g1].rearrange("g p n t -> p g (n t)")[:, :, 4 * n0 : 4 * n1]
            nc.sync.dma_start(out=w_sb[w][:, g0:g1, n0:n1].bitcast(I32), in_=src.bitcast(I32))

        for g0, g1 in ((0, 3), (3, 6)):
            load_words(W_R, g0, g1, 0, N_HID)
        for g0, g1 in ((0, 3), (3, 5), (5, 6)):
            load_words(W_Z, g0, g1, 0, N_HID)
        for g0, g1, n0, n1 in H_LOADS:
            load_words(W_H, g0, g1, n0, n1)

        xw = xh[:].bitcast(F32)
        gw = grouped[:].bitcast(F32)
        pts = []
        for j in range(3):
            pt = bank(4 + j, [P, 2, 2, P], F32, "pt%d" % j)
            for gg in range(2):
                g = 2 * j + gg
                for u in range(2):
                    nc.tensor.transpose(pt[:, gg, u, :], xw[:, 256 * g + u : 256 * (g + 1) : 2], ident_f[:])
            pts.append(pt)

        def copy_xh(j):
            nc.vector.tensor_copy(
                out=gw[:, 512 * j : 512 * (j + 1)].rearrange("p (g r u) -> p g r u", g=2, u=2),
                in_=pts[j][:].rearrange("p g u r -> p g r u"),
            )

        def quant_xh(j):
            nc.vector.quantize_mx(
                out=xh_codes[:, 256 * j : 256 * (j + 1)].bitcast(FP8X4),
                scales=xh_scales[:, 256 * j : 256 * (j + 1)],
                in_=grouped[:, 1024 * j : 1024 * (j + 1)],
            )

        copy_xh(0)
        copy_xh(1)
        quant_xh(0)
        copy_xh(2)
        quant_xh(1)
        quant_xh(2)

        bias_banks = (7, 4, 5, 6, 7, 4)
        for w in range(3):
            for half in range(2):
                pb = bank(bias_banks[2 * w + half], [P, 1024], BF16, "pb%d_%d" % (w, half))
                for s in range(2):
                    col = 1024 * half + 512 * s
                    nc.tensor.matmul(
                        out=pb[:, 512 * s : 512 * (s + 1)],
                        lhsT=ident_b[:, w : w + 1].to_broadcast([P, P]),
                        rhs=staging[:, col : col + 512],
                        start=True,
                        stop=True,
                    )
                nc.scalar.copy(out=bias_bc[w][:, 1024 * half : 1024 * (half + 1)], in_=pb[:])

        def mx_pass(acc, w, g, c, start, stop):
            mx_cols(acc, w, g, c * CHUNK, CHUNK, start, stop)

        def mx_cols(acc, w, g, n0, width, start, stop):
            slot, k = plane_of(w, g)
            if w == W_H and g >= X_GROUPS:
                codes, scl, col = rh_codes, rh_scales, P * (g - X_GROUPS)
            else:
                codes, scl, col = xh_codes, xh_scales, P * g
            nc.tensor.matmul_mx(
                out=acc[:],
                lhsT=codes[:, col : col + P].bitcast(FP8X4),
                lhsT_scale=scl[:, col : col + P],
                rhs=w_sb[w][:, g, n0 : n0 + width].bitcast(FP8X4),
                rhs_scale=planes[k:P, slot * N_HID + n0 : slot * N_HID + n0 + width],
                start=start,
                stop=stop,
            )

        def cols_of(c):
            return slice(c * CHUNK, (c + 1) * CHUNK)

        def add_bias(acc, w, c, shift):
            t = work.tile([P, CHUNK], F32, name="t")
            nc.vector.scalar_tensor_tensor(
                out=t[:], in0=acc[:], scalar=shift, in1=bias_bc[w][:, cols_of(c)], op0=ALU.add, op1=ALU.add
            )
            return t

        nc.scalar.activation(out=hp1[:], in_=xh[:, N_IN:N_CAT], func=ACT.Copy, bias=1.0, scale=1.0)

        r_acc = [bank(c, [P, CHUNK], F32, "r_acc%d" % c) for c in range(CHUNKS)]
        for g in range(GROUPS):
            for c in range(CHUNKS):
                mx_pass(r_acc[c], W_R, g, c, g == 0, g == GROUPS - 1)

        rh = keep.tile([P, CHUNKS, 4, P], BF16, name="rh", tag="stage_rh")
        z_acc = [bank(4 + c, [P, CHUNK], F32, "z_acc%d" % c) for c in range(CHUNKS)]
        r_a = {}
        prh = {}

        def r_front(c):
            t = add_bias(r_acc[c], W_R, c, 3.0)
            a = work.tile([P, 4, P], F32, name="a")
            nc.scalar.activation(
                out=a[:], in_=t[:].rearrange("p (m t) -> p t m", t=4), func=ACT.Relu, scale=1.0 / 6.0
            )
            r_a[c] = a

        def r_back(c):
            nc.vector.scalar_tensor_tensor(
                out=rh[:, c],
                in0=r_a[c][:],
                scalar=1.0,
                in1=xh[:, N_IN + c * CHUNK : N_IN + (c + 1) * CHUNK].rearrange("p (m t) -> p t m", t=4),
                op0=ALU.min,
                op1=ALU.mult,
            )

        def z_group(g):
            for cc in range(CHUNKS):
                mx_pass(z_acc[cc], W_Z, g, cc, g == 0, g == GROUPS - 1)

        def rh_transpose(c):
            prh[c] = bank(c, [P, 4, P], BF16, "prh%d" % c)
            for t4 in range(4):
                nc.tensor.transpose(prh[c][:, t4, :], rh[:, c, t4, :], ident_b[:])

        def rh_copy(c):
            nc.scalar.copy(
                out=rh_grouped[:, 512 * c : 512 * (c + 1)].rearrange("p (r t) -> p r t", t=4),
                in_=prh[c][:].rearrange("p t r -> p r t"),
            )

        def rh_quant(c):
            nc.vector.quantize_mx(
                out=rh_codes[:, P * c : P * (c + 1)].bitcast(FP8X4),
                scales=rh_scales[:, P * c : P * (c + 1)],
                in_=rh_grouped[:, 512 * c : 512 * (c + 1)],
            )

        r_front(0)
        r_front(1)
        r_back(0)
        z_group(0)
        rh_transpose(0)
        r_front(2)
        rh_copy(0)
        r_back(1)
        z_group(1)
        rh_transpose(1)
        r_front(3)
        rh_copy(1)
        r_back(2)
        rh_quant(0)
        z_group(2)
        rh_transpose(2)
        rh_copy(2)
        r_back(3)
        rh_quant(1)
        z_group(3)
        rh_transpose(3)
        rh_copy(3)
        rh_quant(2)
        rh_quant(3)
        z_group(4)
        z_group(5)

        z_a = {}

        def z_front(c):
            t = add_bias(z_acc[c], W_Z, c, 3.0)
            a = work.tile([P, CHUNK], F32, name="a")
            nc.scalar.activation(out=a[:], in_=t[:], func=ACT.Relu, scale=1.0 / 6.0)
            z_a[c] = a

        def z_back(c):
            nc.vector.scalar_tensor_tensor(
                out=zhp[:, cols_of(c)], in0=z_a[c][:], scalar=1.0, in1=hp1[:, cols_of(c)], op0=ALU.min, op1=ALU.mult
            )
            nc.scalar.activation(out=omz[:, cols_of(c)], in_=z_a[c][:], func=ACT.Relu, bias=1.0, scale=-1.0)

        z_front(0)
        z_front(1)
        z_back(0)
        z_front(2)
        z_back(1)
        z_front(3)
        z_back(2)
        z_back(3)

        h_acc = [bank(i, [P, width], F32, "h_acc%d" % i) for i, (n0, width) in enumerate(H_CHUNKS)]
        h_a = {}

        def h_passes(chunks):
            for g in range(GROUPS):
                for i in chunks:
                    n0, width = H_CHUNKS[i]
                    mx_cols(h_acc[i], W_H, g, n0, width, g == 0, g == GROUPS - 1)

        def h_front(j):
            i, n0, width = H_PIECES[j]
            off = n0 - H_CHUNKS[i][0]
            t = work.tile([P, width], F32, name="t")
            nc.vector.scalar_tensor_tensor(
                out=t[:], in0=h_acc[i][:, off : off + width], scalar=1.0, in1=bias_bc[W_H][:, n0 : n0 + width],
                op0=ALU.add, op1=ALU.add
            )
            a = work.tile([P, width], F32, name="a")
            nc.scalar.activation(out=a[:], in_=t[:], func=ACT.Relu)
            h_a[j] = a

        def h_mid(j):
            i, n0, width = H_PIECES[j]
            nc.vector.scalar_tensor_tensor(
                out=h_a[j][:], in0=h_a[j][:], scalar=2.0, in1=omz[:, n0 : n0 + width], op0=ALU.min, op1=ALU.mult
            )

        def h_back(j):
            i, n0, width = H_PIECES[j]
            nc.vector.scalar_tensor_tensor(
                out=zhp[:, n0 : n0 + width], in0=h_a[j][:], scalar=-1.0, in1=zhp[:, n0 : n0 + width],
                op0=ALU.add, op1=ALU.add
            )

        def h_store(n0, width):
            nc.sync.dma_start(out=out[:, n0 : n0 + width], in_=zhp[:, n0 : n0 + width])

        for i in range(4):
            h_passes((i,) if i < 3 else (3, 4))
            h_front(2 * i)
            h_front(2 * i + 1)
            h_mid(2 * i)
            h_mid(2 * i + 1)
            h_back(2 * i)
            h_back(2 * i + 1)
            h_store(512 * i, 512)
